import numpy as np
import ml_dtypes


def mxq(x, axis, fmt="e4m3"):
    dtype, down = {"e4m3": (ml_dtypes.float8_e4m3fn, 7), "e5m2": (ml_dtypes.float8_e5m2, 14)}[fmt]
    v = np.moveaxis(np.asarray(x, np.float32).astype(ml_dtypes.bfloat16).astype(np.float64), axis, -1)
    blocks = v.reshape(v.shape[:-1] + (-1, 32))
    amax = np.abs(blocks).max(-1, keepdims=True)
    byte = np.maximum(np.where(amax > 0, np.frexp(amax)[1] - 1 + 127, 0) - down, 1)
    scale = np.exp2(byte - 127.0)
    codes = (blocks / scale).astype(np.float32).astype(dtype).astype(np.float64)
    return np.moveaxis((codes * scale).reshape(v.shape), -1, axis)


WIDE = False


def mx_kscale(k):
    if not WIDE:
        return np.ones(k)
    levels = np.array([10, -10, 5, -5, 0])
    if k % 512:
        return np.exp2(np.random.permutation(np.resize(levels, k // 32))).repeat(32)
    a = np.empty((k // 512, 16))
    for p in range(k // 512):
        a[p, :8] = np.random.permutation(np.resize(levels, 8))
        for g in range(8):
            far = levels[np.abs(levels - a[p, g]) >= 10]
            a[p, g + 8] = far[np.random.randint(len(far))]
    return np.exp2(a.ravel()).repeat(32)


BF16 = ml_dtypes.bfloat16


def bf(x):
    return np.asarray(x, np.float32).astype(BF16)


def f64(x):
    return np.asarray(x).astype(np.float64)


B, CI, C, N = 3, 512, 512, 1024
T = B * N
EPS = 1e-5
QS = np.sqrt(2.0) / C ** 0.25


def norm_stats(x):
    mu = x.mean(-1)
    var = np.square(x - mu[:, :, None]).mean(-1)
    return mu, 1.0 / np.sqrt(var + EPS)


def setup_inputs():
    k = mx_kscale(T)
    s = (k / k.min()).reshape(B, 1, N)
    u = mx_kscale(C)
    a = np.exp2(np.random.uniform(-8.0, 1.0, (CI, 1)))
    q0 = bf(a * (np.random.standard_normal((B, CI, N)) + 0.5 * np.random.standard_normal((B, CI, 1))))
    w0 = bf(np.random.standard_normal((C, CI)) * QS / np.sqrt(CI))
    bq = bf(np.random.standard_normal(C) * 0.3 * QS)
    g = bf(np.random.standard_normal((B, C, N)) * np.exp2(np.random.randint(-6, 1, (B, 1, N))) / s * u[None, :, None])
    mu, rstd = norm_stats(f64(q0))
    return {"q": bf(f64(q0) * s), "Wq": bf(f64(w0) / u[:, None]), "bq": bq,
            "mu": np.asarray(mu, np.float32), "rstd": np.asarray(rstd, np.float32), "grad_out": g}


def reference(q, Wq, bq, mu, rstd, grad_out):
    r = f64(rstd)[:, :, None]
    xn = (f64(q) - f64(mu)[:, :, None]) * r
    g = f64(grad_out).transpose(1, 0, 2).reshape(C, T)
    xt = xn.transpose(1, 0, 2).reshape(CI, T)
    dxt = mxq(f64(Wq), 0, "e4m3").T @ mxq(g, 0, "e5m2")
    dxn = dxt.reshape(CI, B, N).transpose(1, 0, 2)
    m1 = dxn.mean(-1, keepdims=True)
    m2 = (dxn * xn).mean(-1, keepdims=True)
    dq = r * (dxn - m1 - xn * m2)
    dWq = mxq(g, 1, "e5m2") @ mxq(xt, 1, "e4m3").T
    return dq, dWq

@@ -1,0 +1,332 @@
+from contextlib import ExitStack
+
+import concourse.mybir as mybir
+from concourse.masks import make_identity
+
+B, CI, CO, N = 3, 512, 512, 1024
+FLOPS = 2 * 2 * CO * CI * B * N
+BYTES = 2 * (2 * B * CI * N + CO * CI) + 4 * (2 * B * CI + B * CI * N + CO * CI)
+
+F32 = mybir.dt.float32
+BF16 = mybir.dt.bfloat16
+U32 = mybir.dt.uint32
+U8 = mybir.dt.uint8
+E4 = mybir.dt.float8_e4m3fn_x4
+E5 = mybir.dt.float8_e5m2_x4
+ADD = mybir.AluOpType.add
+SUB = mybir.AluOpType.subtract
+MULT = mybir.AluOpType.mult
+IDENT = mybir.ActivationFunctionType.Identity
+
+P = 128
+J = 4
+HALF = 512
+TILES = B * J
+V_COLS = 320
+
+
+def tile_adaattn3dstylizer_pa_v_kernel(tc, q, Wq, bq, mu, rstd, grad_out, out_0, out_1):
+    nc = tc.nc
+    with ExitStack() as ctx:
+        keep = ctx.enter_context(tc.tile_pool(name="keep", bufs=1))
+        work = ctx.enter_context(tc.tile_pool(name="work", bufs=3))
+        psum_d = ctx.enter_context(tc.psum_pool(name="psum_d", bufs=4))
+        psum_t = ctx.enter_context(tc.psum_pool(name="psum_t", bufs=3))
+        psum_s = ctx.enter_context(tc.psum_pool(name="psum_s", bufs=1))
+        ctx.enter_context(tc.manual_schedule())
+
+        g_half = {}
+        for h in range(2):
+            g_half[(0, h)] = keep.tile([P, J, HALF], BF16, name="g0%d" % h, align_bytes=64)
+        for b in range(1, B):
+            g_all = keep.tile([P, J, N], BF16, name="g%d" % b, align_bytes=64)
+            for h in range(2):
+                g_half[(b, h)] = g_all[:, :, h * HALF : (h + 1) * HALF]
+            g_half[b] = g_all
+        q_sb = [keep.tile([P, J, N], BF16, name="q%d" % b, align_bytes=64) for b in range(B)]
+        w_sb = keep.tile([P, J, CI], BF16, name="w_sb", align_bytes=64)
+        mu_sb = keep.tile([P, TILES], F32, name="mu_sb")
+        rs_sb = keep.tile([P, TILES], F32, name="rs_sb")
+        g_view = [grad_out[b].rearrange("(p j) n -> p j n", j=J) for b in range(B)]
+        q_view = [q[b].rearrange("(p j) n -> p j n", j=J) for b in range(B)]
+        nc.scalar.dma_start(out=rs_sb[:].rearrange("p (b j) -> p b j", j=J), in_=rstd.rearrange("b (p j) -> p b j", j=J))
+        nc.scalar.dma_start(out=mu_sb[:].rearrange("p (b j) -> p b j", j=J), in_=mu.rearrange("b (p j) -> p b j", j=J))
+        nc.sync.dma_start(out=g_half[(0, 0)][:], in_=g_view[0][:, :, 0:HALF])
+        nc.sync.dma_start(out=w_sb[:], in_=Wq.rearrange("(p j) i -> p j i", j=J))
+        nc.sync.dma_start(out=g_half[(0, 1)][:], in_=g_view[0][:, :, HALF:N])
+        nc.sync.dma_start(out=q_sb[0][:], in_=q_view[0])
+        for b in range(1, B):
+            nc.sync.dma_start(out=g_half[b][:], in_=g_view[b])
+            nc.sync.dma_start(out=q_sb[b][:], in_=q_view[b])
+
+        warm = keep.tile([P, 1], F32, name="warm")
+        nc.vector.memset(warm[:], 0.0)
+        nc.scalar.activation(out=warm[:], in_=warm[:], func=IDENT)
+        neg_inv_n = keep.tile([P, 1], F32, name="neg_inv_n")
+        nc.vector.memset(neg_inv_n[:], -1.0 / N)
+        ident = keep.tile([P, P], F32, name="ident")
+        make_identity(nc, ident[:])
+        sq = keep.tile([P, TILES], F32, name="sq")
+        c3 = keep.tile([P, TILES], F32, name="c3")
+        e3 = keep.tile([P, TILES], F32, name="e3")
+        neg_mu = keep.tile([P, TILES], F32, name="neg_mu")
+        nc.vector.tensor_tensor(out=sq[:], in0=rs_sb[:], in1=rs_sb[:], op=MULT)
+        nc.vector.tensor_scalar(out=neg_mu[:], in0=mu_sb[:], scalar1=-1.0, scalar2=None, op0=MULT)
+        nc.vector.scalar_tensor_tensor(out=c3[:], in0=sq[:], scalar=-1.0 / N, in1=rs_sb[:], op0=MULT, op1=MULT)
+        nc.vector.scalar_tensor_tensor(out=e3[:], in0=c3[:], scalar=float(N), in1=mu_sb[:], op0=MULT, op1=MULT)
+
+        w_codes = keep.tile([P, CI], U32, name="w_codes", align_bytes=64)
+        w_scales = keep.tile([P, CI], U8, name="w_scales", align_bytes=64)
+        go_codes = [keep.tile([P, N], U32, name="go_codes%d" % b, align_bytes=64) for b in range(B)]
+        go_scales = [keep.tile([P, N], U8, name="go_scales%d" % b, align_bytes=64) for b in range(B)]
+        gt_codes = [keep.tile([P, CO], U32, name="gt_codes%d" % k, align_bytes=64) for k in range(2 * B)]
+        gt_scales = [keep.tile([P, CO], U8, name="gt_scales%d" % k, align_bytes=64) for k in range(2 * B)]
+        xt_codes = [keep.tile([P, CI], U32, name="xt_codes%d" % k, align_bytes=64) for k in range(2 * B)]
+        xt_scales = [keep.tile([P, CI], U8, name="xt_scales%d" % k, align_bytes=64) for k in range(2 * B)]
+        x_sb = {}
+        grouped = {}
+
+        def copy(engine, out, in_):
+            if engine == "V":
+                nc.vector.tensor_copy(out=out, in_=in_)
+            else:
+                nc.scalar.copy(out=out, in_=in_)
+
+        def interleave_g(engine, b, h, c0, c1):
+            if (b, h) not in grouped:
+                grouped[(b, h)] = work.tile([P, HALF, J], BF16, name="go", bufs=2, align_bytes=64)
+            dst = grouped[(b, h)][:, c0:c1, :].rearrange("p (c i) t -> p c t i", i=4)
+            src = g_half[(b, h)][:, :, c0:c1].rearrange("p t (c i) -> p c t i", i=4)
+            copy(engine, dst, src)
+
+        def quantize_go(b, h):
+            cols = slice(h * HALF, (h + 1) * HALF)
+            nc.vector.quantize_mx(out=go_codes[b][:, cols].bitcast(E5), scales=go_scales[b][:, cols],
+                                  in_=grouped[(b, h)][:].rearrange("p c t -> p (c t)"))
+
+        w_grouped = keep.tile([P, J, P, J], BF16, name="w_grouped", align_bytes=64)
+
+        def interleave_w(engine, j0, j1):
+            copy(engine, w_grouped[:, j0:j1], w_sb[:].rearrange("p t (m j) -> p j m t", j=J)[:, j0:j1])
+
+        def make_x(b, j):
+            if b not in x_sb:
+                x_sb[b] = work.tile([P, J, N], BF16, name="x", bufs=2, align_bytes=64)
+            col = slice(b * J + j, b * J + j + 1)
+            nc.vector.tensor_scalar(out=x_sb[b][:, j, :], in0=q_sb[b][:, j, :], scalar1=mu_sb[:, col], scalar2=rs_sb[:, col], op0=SUB, op1=MULT)
+
+        turned = {}
+
+        def transpose_pair(kind, b, h, pair):
+            bank = psum_t.tile([P, 2, 2, P], F32, name="bank")
+            for jj in range(2):
+                rows = g_half[(b, h)][:, 2 * pair + jj, :] if kind == "g" else x_sb[b][:, 2 * pair + jj, h * HALF : (h + 1) * HALF]
+                for u in range(2):
+                    nc.tensor.transpose(bank[:, jj, u, :], rows.bitcast(F32)[:, u::2], ident[:])
+            turned[(kind, b, h, pair)] = bank
+
+        def copy_pair(engine, kind, b, h, pair):
+            if (kind, b, h) not in grouped:
+                grouped[(kind, b, h)] = work.tile([P, CO, J], BF16, name="tt", bufs=4, align_bytes=64)
+            dst = grouped[(kind, b, h)][:].rearrange("p c t -> p (c t)").bitcast(F32)[:, pair * 512 : (pair + 1) * 512]
+            copy(engine, dst.rearrange("p (j r u) -> p j r u", j=2, u=2), turned[(kind, b, h, pair)][:].rearrange("p j u r -> p j r u"))
+
+        def quantize_t(kind, b, h):
+            k = 2 * b + h
+            codes, scales, fmt = (gt_codes[k], gt_scales[k], E5) if kind == "g" else (xt_codes[k], xt_scales[k], E4)
+            nc.vector.quantize_mx(out=codes[:].bitcast(fmt), scales=scales[:], in_=grouped[(kind, b, h)][:].rearrange("p c t -> p (c t)"))
+
+        neg_m1 = {}
+        d3 = {}
+        r1 = {}
+
+        acc_of = {}
+
+        def sum_products(b, h):
+            if h == 0:
+                acc_of[b] = psum_s.tile([P, CI], F32, name="acc")
+            for k in range(h * J, (h + 1) * J):
+                cols = slice(k * P, (k + 1) * P)
+                nc.tensor.matmul_mx(out=acc_of[b][:], lhsT=go_codes[b][:, cols].bitcast(E5), lhsT_scale=go_scales[b][:, cols],
+                                    rhs=w_codes[:].bitcast(E4), rhs_scale=w_scales[:], start=(k == 0), stop=(k == 2 * J - 1))
+
+        part_of = {}
+
+        def copy_sums(b):
+            part_of[b] = work.tile([P, CI], F32, name="part", bufs=1)
+            nc.scalar.copy(out=part_of[b][:], in_=acc_of[b][:])
+
+        def mean(b):
+            neg_m1[b] = psum_s.tile([P, J], F32, name="acc")
+            for j in range(J):
+                nc.tensor.matmul(out=neg_m1[b][:, j : j + 1], lhsT=part_of[b][:, j * P : (j + 1) * P], rhs=neg_inv_n[:], start=True, stop=True)
+
+        def mean_terms(b):
+            cols = slice(b * J, (b + 1) * J)
+            d3[b] = work.tile([P, J], F32, name="d3", bufs=2)
+            r1[b] = work.tile([P, J], F32, name="r1", bufs=2)
+            nc.vector.tensor_tensor(out=d3[b][:], in0=neg_m1[b][:], in1=e3[:, cols], op=MULT)
+            nc.vector.tensor_tensor(out=r1[b][:], in0=neg_m1[b][:], in1=rs_sb[:, cols], op=MULT)
+
+        dxn = {}
+        s2 = {}
+        ab = {}
+        lin = {}
+
+        def project(t):
+            b, j = divmod(t, J)
+            for h in range(2):
+                d = psum_d.tile([P, HALF], F32, name="d")
+                nc.tensor.matmul_mx(out=d[:], lhsT=w_codes[:, j * P : (j + 1) * P].bitcast(E4), lhsT_scale=w_scales[:, j * P : (j + 1) * P],
+                                    rhs=go_codes[b][:, h * HALF : (h + 1) * HALF].bitcast(E5), rhs_scale=go_scales[b][:, h * HALF : (h + 1) * HALF],
+                                    start=True, stop=True)
+                dxn[(t, h)] = d
+
+        def second_moment(t):
+            b, j = divmod(t, J)
+            s2[t] = work.tile([P, 2], F32, name="s2")
+            for h in range(2):
+                junk = work.tile([P, HALF], F32, name="junk", bufs=2)
+                nc.vector.scalar_tensor_tensor(out=junk[:], in0=dxn[(t, h)][:], scalar=c3[:, t : t + 1], in1=q_sb[b][:, j, h * HALF : (h + 1) * HALF],
+                                               op0=MULT, op1=MULT, accum_out=s2[t][:, h : h + 1])
+
+        def line(t):
+            b, j = divmod(t, J)
+            ab[t] = work.tile([P, 2], F32, name="ab")
+            nc.gpsimd.tensor_scalar(out=ab[t][:, 0:1], in0=s2[t][:, 0:1], scalar1=s2[t][:, 1:2], scalar2=d3[b][:, j : j + 1], op0=ADD, op1=ADD)
+            nc.gpsimd.tensor_scalar(out=ab[t][:, 1:2], in0=ab[t][:, 0:1], scalar1=neg_mu[:, t : t + 1], scalar2=r1[b][:, j : j + 1], op0=MULT, op1=ADD)
+
+        def linear_term(t, halves="SS"):
+            b, j = divmod(t, J)
+            lin[t] = work.tile([P, N], F32, name="lin")
+            if halves == "SS":
+                nc.scalar.activation(out=lin[t][:], in_=q_sb[b][:, j, :], func=IDENT, scale=ab[t][:, 0:1], bias=ab[t][:, 1:2])
+            else:
+                for h, e in enumerate(halves):
+                    cols = slice(h * HALF, (h + 1) * HALF)
+                    if e == "S":
+                        nc.scalar.activation(out=lin[t][:, cols], in_=q_sb[b][:, j, cols], func=IDENT, scale=ab[t][:, 0:1], bias=ab[t][:, 1:2])
+                    else:
+                        nc.vector.tensor_scalar(out=lin[t][:, cols], in0=q_sb[b][:, j, cols], scalar1=ab[t][:, 0:1], scalar2=ab[t][:, 1:2], op0=MULT, op1=ADD)
+
+        def finish(t, split=False):
+            b, j = divmod(t, J)
+            res = work.tile([P, N], F32, name="res")
+            out_rows = out_0[b].rearrange("(p j) n -> p j n", j=J)[:, j, :]
+            for h in range(2):
+                cols = slice(h * HALF, (h + 1) * HALF)
+                nc.vector.scalar_tensor_tensor(out=res[:, cols], in0=dxn[(t, h)][:], scalar=rs_sb[:, t : t + 1], in1=lin[t][:, cols], op0=MULT, op1=ADD)
+                if split:
+                    nc.sync.dma_start(out=out_rows[:, cols], in_=res[:, cols])
+            if not split:
+                nc.sync.dma_start(out=out_rows, in_=res[:])
+
+        wacc = {}
+
+        def weight_grad(j):
+            acc = psum_t.tile([P, CI], F32, name="bank")
+            for k in range(2 * B):
+                cols = slice(j * P, (j + 1) * P)
+                nc.tensor.matmul_mx(out=acc[:], lhsT=gt_codes[k][:, cols].bitcast(E5), lhsT_scale=gt_scales[k][:, cols],
+                                    rhs=xt_codes[k][:].bitcast(E4), rhs_scale=xt_scales[k][:], start=(k == 0), stop=(k == 2 * B - 1))
+            wacc[j] = acc
+
+        def store_weight_grad(engine, j):
+            res = work.tile([P, CI], F32, name="wres", bufs=4)
+            copy(engine, res[:].rearrange("p (m j) -> p m j", j=J), wacc[j][:].rearrange("p (j m) -> p m j", j=J))
+            nc.sync.dma_start(out=out_1.rearrange("(p j) i -> p j i", j=J)[:, j, :], in_=res[:])
+
+        interleave_g("V", 0, 0, 0, V_COLS)
+        interleave_g("S", 0, 0, V_COLS, HALF)
+        transpose_pair("g", 0, 0, 0)
+        transpose_pair("g", 0, 0, 1)
+        interleave_w("V", 0, 3)
+        interleave_w("S", 3, 4)
+        quantize_go(0, 0)
+        copy_pair("S", "g", 0, 0, 0)
+        interleave_g("V", 0, 1, 0, V_COLS)
+        interleave_g("S", 0, 1, V_COLS, HALF)
+        nc.vector.quantize_mx(out=w_codes[:].bitcast(E4), scales=w_scales[:], in_=w_grouped[:].rearrange("p j m t -> p (j m t)"))
+        transpose_pair("g", 0, 1, 0)
+        copy_pair("S", "g", 0, 0, 1)
+        transpose_pair("g", 0, 1, 1)
+        sum_products(0, 0)
+        quantize_go(0, 1)
+        sum_products(0, 1)
+        copy_pair("S", "g", 0, 1, 0)
+        copy_pair("S", "g", 0, 1, 1)
+        project(0)
+        make_x(0, 0)
+        make_x(0, 1)
+        quantize_t("g", 0, 0)
+        make_x(0, 2)
+        make_x(0, 3)
+        quantize_t("g", 0, 1)
+        copy_sums(0)
+        interleave_g("V", 1, 0, 0, HALF)
+        project(1)
+        transpose_pair("x", 0, 0, 0)
+        mean(0)
+        transpose_pair("x", 0, 0, 1)
+        copy_pair("S", "x", 0, 0, 0)
+        copy_pair("S", "x", 0, 0, 1)
+
+        turn_at = {0: [("x", 0, 1)], 1: [("g", 1, 0)], 2: [("g", 1, 1)], 3: [("x", 1, 0)], 4: [("x", 1, 1)], 5: [("g", 2, 0)], 6: [("g", 2, 1), ("x", 2, 0)], 7: [("x", 2, 1)]}
+        quarters = {0: [(1, 2)], 1: [(1, 3)], 2: [(2, 0)], 3: [(2, 1)], 4: [(2, 2)], 5: [(2, 3)]}
+        quantize_at = {0: (1, 0), 2: (1, 1), 4: (2, 0), 6: (2, 1)}
+        x_at = {0: (1, 0), 1: (1, 2), 4: (2, 0), 5: (2, 2)}
+        sums_at = (3, 7)
+        lin_e = ["SS"] * 11 + ["SV"]
+        wg_at = {8: [0], 9: [1], 10: [2], 11: [3]}
+        swg_at = {9: [0], 10: [1], 11: [2]}
+        for t in range(TILES):
+            b, j = divmod(t, J)
+            units = turn_at.get(t, [])
+            if t in sums_at:
+                copy_sums(b + 1)
+            for unit in units:
+                for pair in range(2):
+                    transpose_pair(*unit, pair)
+                    if t > 0:
+                        copy_pair("S", *unit, pair)
+            second_moment(t)
+            if t == 0:
+                quantize_go(1, 0)
+                sum_products(1, 0)
+                make_x(1, 0)
+                make_x(1, 1)
+            if t > 0 and j == 0:
+                finish(t - 1)
+            if j == 0:
+                mean_terms(b)
+            line(t)
+            if j > 0:
+                finish(t - 1)
+            linear_term(t, lin_e[t])
+            if t == 0:
+                for unit in units:
+                    for pair in range(2):
+                        copy_pair("S", *unit, pair)
+            for gb, k in quarters.get(t, []):
+                interleave_g("S", gb, k // 2, (k % 2) * HALF // 2, (k % 2 + 1) * HALF // 2)
+            if 0 < t < TILES - 1:
+                project(t + 1)
+            if t in sums_at:
+                mean(b + 1)
+            if t == 1:
+                quantize_t("x", 0, 0)
+            for unit in turn_at.get(t - 1, []):
+                quantize_t(*unit)
+            if t in quantize_at and t > 0:
+                quantize_go(*quantize_at[t])
+                sum_products(*quantize_at[t])
+            if t in x_at and t > 0:
+                xb, xj = x_at[t]
+                make_x(xb, xj)
+                make_x(xb, xj + 1)
+            for k in wg_at.get(t, []):
+                weight_grad(k)
+            for k in swg_at.get(t, []):
+                store_weight_grad("S", k)
+        finish(TILES - 1, split=True)
+        store_weight_grad("S", 3)

@@ -49,11 +49,11 @@ def tile_adaattn3dstylizer_pa_v_kernel(tc, q, Wq, bq, mu, rstd, grad_out, out_0,
         rs_sb = keep.tile([P, TILES], F32, name="rs_sb")
         g_view = [grad_out[b].rearrange("(p j) n -> p j n", j=J) for b in range(B)]
         q_view = [q[b].rearrange("(p j) n -> p j n", j=J) for b in range(B)]
-        nc.scalar.dma_start(out=rs_sb[:].rearrange("p (b j) -> p b j", j=J), in_=rstd.rearrange("b (p j) -> p b j", j=J))
-        nc.scalar.dma_start(out=mu_sb[:].rearrange("p (b j) -> p b j", j=J), in_=mu.rearrange("b (p j) -> p b j", j=J))
         nc.sync.dma_start(out=g_half[(0, 0)][:], in_=g_view[0][:, :, 0:HALF])
         nc.sync.dma_start(out=w_sb[:], in_=Wq.rearrange("(p j) i -> p j i", j=J))
         nc.sync.dma_start(out=g_half[(0, 1)][:], in_=g_view[0][:, :, HALF:N])
+        nc.sync.dma_start(out=rs_sb[:].rearrange("p (b j) -> p b j", j=J), in_=rstd.rearrange("b (p j) -> p b j", j=J))
+        nc.sync.dma_start(out=mu_sb[:].rearrange("p (b j) -> p b j", j=J), in_=mu.rearrange("b (p j) -> p b j", j=J))
         nc.sync.dma_start(out=q_sb[0][:], in_=q_view[0])
         for b in range(1, B):
             nc.sync.dma_start(out=g_half[b][:], in_=g_view[b])
@@ -70,10 +70,12 @@ def tile_adaattn3dstylizer_pa_v_kernel(tc, q, Wq, bq, mu, rstd, grad_out, out_0,
         c3 = keep.tile([P, TILES], F32, name="c3")
         e3 = keep.tile([P, TILES], F32, name="e3")
         neg_mu = keep.tile([P, TILES], F32, name="neg_mu")
-        nc.vector.tensor_tensor(out=sq[:], in0=rs_sb[:], in1=rs_sb[:], op=MULT)
-        nc.vector.tensor_scalar(out=neg_mu[:], in0=mu_sb[:], scalar1=-1.0, scalar2=None, op0=MULT)
-        nc.vector.scalar_tensor_tensor(out=c3[:], in0=sq[:], scalar=-1.0 / N, in1=rs_sb[:], op0=MULT, op1=MULT)
-        nc.vector.scalar_tensor_tensor(out=e3[:], in0=c3[:], scalar=float(N), in1=mu_sb[:], op0=MULT, op1=MULT)
+
+        def channel_constants():
+            nc.vector.tensor_tensor(out=sq[:], in0=rs_sb[:], in1=rs_sb[:], op=MULT)
+            nc.vector.tensor_scalar(out=neg_mu[:], in0=mu_sb[:], scalar1=-1.0, scalar2=None, op0=MULT)
+            nc.vector.scalar_tensor_tensor(out=c3[:], in0=sq[:], scalar=-1.0 / N, in1=rs_sb[:], op0=MULT, op1=MULT)
+            nc.vector.scalar_tensor_tensor(out=e3[:], in0=c3[:], scalar=float(N), in1=mu_sb[:], op0=MULT, op1=MULT)
 
         w_codes = keep.tile([P, CI], U32, name="w_codes", align_bytes=64)
         w_scales = keep.tile([P, CI], U8, name="w_scales", align_bytes=64)
@@ -142,13 +144,14 @@ def tile_adaattn3dstylizer_pa_v_kernel(tc, q, Wq, bq, mu, rstd, grad_out, out_0,
 
         acc_of = {}
 
-        def sum_products(b, h):
-            if h == 0:
-                acc_of[b] = psum_s.tile([P, CI], F32, name="acc")
-            for k in range(h * J, (h + 1) * J):
-                cols = slice(k * P, (k + 1) * P)
-                nc.tensor.matmul_mx(out=acc_of[b][:], lhsT=go_codes[b][:, cols].bitcast(E5), lhsT_scale=go_scales[b][:, cols],
-                                    rhs=w_codes[:].bitcast(E4), rhs_scale=w_scales[:], start=(k == 0), stop=(k == 2 * J - 1))
+        def sum_products(b, pairs):
+            for i in pairs:
+                if i == 0:
+                    acc_of[b] = psum_s.tile([P, CI], F32, name="acc")
+                for k in (2 * i, 2 * i + 1):
+                    cols = slice(k * P, (k + 1) * P)
+                    nc.tensor.matmul_mx(out=acc_of[b][:], lhsT=go_codes[b][:, cols].bitcast(E5), lhsT_scale=go_scales[b][:, cols],
+                                        rhs=w_codes[:].bitcast(E4), rhs_scale=w_scales[:], start=(k == 0), stop=(k == 2 * J - 1))
 
         part_of = {}
 
@@ -236,6 +239,12 @@ def tile_adaattn3dstylizer_pa_v_kernel(tc, q, Wq, bq, mu, rstd, grad_out, out_0,
             copy(engine, res[:].rearrange("p (m j) -> p m j", j=J), wacc[j][:].rearrange("p (j m) -> p m j", j=J))
             nc.sync.dma_start(out=out_1.rearrange("(p j) i -> p j i", j=J)[:, j, :], in_=res[:])
 
+        def keep_clock(n):
+            spare = psum_t.tile([P, HALF], F32, name="bank")
+            for k in range(n):
+                nc.tensor.matmul_mx(out=spare[:], lhsT=w_codes[:, 0:P].bitcast(E4), lhsT_scale=w_scales[:, 0:P],
+                                    rhs=go_codes[0][:, 0:HALF].bitcast(E5), rhs_scale=go_scales[0][:, 0:HALF], start=True, stop=True)
+
         interleave_g("V", 0, 0, 0, V_COLS)
         interleave_g("S", 0, 0, V_COLS, HALF)
         transpose_pair("g", 0, 0, 0)
@@ -250,9 +259,9 @@ def tile_adaattn3dstylizer_pa_v_kernel(tc, q, Wq, bq, mu, rstd, grad_out, out_0,
         transpose_pair("g", 0, 1, 0)
         copy_pair("S", "g", 0, 0, 1)
         transpose_pair("g", 0, 1, 1)
-        sum_products(0, 0)
+        sum_products(0, (0, 1))
         quantize_go(0, 1)
-        sum_products(0, 1)
+        sum_products(0, (2, 3))
         copy_pair("S", "g", 0, 1, 0)
         copy_pair("S", "g", 0, 1, 1)
         project(0)
@@ -261,9 +270,11 @@ def tile_adaattn3dstylizer_pa_v_kernel(tc, q, Wq, bq, mu, rstd, grad_out, out_0,
         quantize_t("g", 0, 0)
         make_x(0, 2)
         make_x(0, 3)
+        channel_constants()
         quantize_t("g", 0, 1)
         copy_sums(0)
         interleave_g("V", 1, 0, 0, HALF)
+        interleave_g("S", 1, 1, 0, HALF // 2)
         project(1)
         transpose_pair("x", 0, 0, 0)
         mean(0)
@@ -272,27 +283,28 @@ def tile_adaattn3dstylizer_pa_v_kernel(tc, q, Wq, bq, mu, rstd, grad_out, out_0,
         copy_pair("S", "x", 0, 0, 1)
 
         turn_at = {0: [("x", 0, 1)], 1: [("g", 1, 0)], 2: [("g", 1, 1)], 3: [("x", 1, 0)], 4: [("x", 1, 1)], 5: [("g", 2, 0)], 6: [("g", 2, 1), ("x", 2, 0)], 7: [("x", 2, 1)]}
-        quarters = {0: [(1, 2)], 1: [(1, 3)], 2: [(2, 0)], 3: [(2, 1)], 4: [(2, 2)], 5: [(2, 3)]}
-        quantize_at = {0: (1, 0), 2: (1, 1), 4: (2, 0), 6: (2, 1)}
-        x_at = {0: (1, 0), 1: (1, 2), 4: (2, 0), 5: (2, 2)}
-        sums_at = (3, 7)
+        quarters = {0: [(1, 3)], 1: [(2, 0)], 2: [(2, 1)], 3: [(2, 2)], 4: [(2, 3)]}
+        quantize_at = {0: (1, 0), 1: (1, 1), 3: (2, 0), 5: (2, 1)}
+        x_at = {0: (1, 0), 2: (1, 2), 4: (2, 0), 5: (2, 2)}
         lin_e = ["SS"] * 11 + ["SV"]
         wg_at = {8: [0], 9: [1], 10: [2], 11: [3]}
         swg_at = {9: [0], 10: [1], 11: [2]}
         for t in range(TILES):
             b, j = divmod(t, J)
             units = turn_at.get(t, [])
-            if t in sums_at:
-                copy_sums(b + 1)
-            for unit in units:
-                for pair in range(2):
+            for n, (unit, pair) in enumerate([(unit, pair) for unit in units for pair in range(2)]):
+                if n < 1 or t == 0:
                     transpose_pair(*unit, pair)
                     if t > 0:
                         copy_pair("S", *unit, pair)
+                if n == 0 and t > 0 and b + 1 < B:
+                    sum_products(b + 1, (j,))
+            if t in range(8):
+                keep_clock(1)
             second_moment(t)
             if t == 0:
                 quantize_go(1, 0)
-                sum_products(1, 0)
+                sum_products(1, (0,))
                 make_x(1, 0)
                 make_x(1, 1)
             if t > 0 and j == 0:
@@ -302,6 +314,8 @@ def tile_adaattn3dstylizer_pa_v_kernel(tc, q, Wq, bq, mu, rstd, grad_out, out_0,
             line(t)
             if j > 0:
                 finish(t - 1)
+            if b + 1 < B and j == 3:
+                copy_sums(b + 1)
             linear_term(t, lin_e[t])
             if t == 0:
                 for unit in units:
@@ -311,7 +325,13 @@ def tile_adaattn3dstylizer_pa_v_kernel(tc, q, Wq, bq, mu, rstd, grad_out, out_0,
                 interleave_g("S", gb, k // 2, (k % 2) * HALF // 2, (k % 2 + 1) * HALF // 2)
             if 0 < t < TILES - 1:
                 project(t + 1)
-            if t in sums_at:
+            if t in range(1, 8):
+                keep_clock(1)
+            for unit, pair in [(unit, pair) for unit in units for pair in range(2)][1:]:
+                if t > 0:
+                    transpose_pair(*unit, pair)
+                    copy_pair("S", *unit, pair)
+            if b + 1 < B and j == 3:
                 mean(b + 1)
             if t == 1:
                 quantize_t("x", 0, 0)
@@ -319,7 +339,6 @@ def tile_adaattn3dstylizer_pa_v_kernel(tc, q, Wq, bq, mu, rstd, grad_out, out_0,
                 quantize_t(*unit)
             if t in quantize_at and t > 0:
                 quantize_go(*quantize_at[t])
-                sum_products(*quantize_at[t])
             if t in x_at and t > 0:
                 xb, xj = x_at[t]
                 make_x(xb, xj)

@@ -68,14 +68,10 @@ def tile_adaattn3dstylizer_pa_v_kernel(tc, q, Wq, bq, mu, rstd, grad_out, out_0,
         make_identity(nc, ident[:])
         sq = keep.tile([P, TILES], F32, name="sq")
         c3 = keep.tile([P, TILES], F32, name="c3")
-        e3 = keep.tile([P, TILES], F32, name="e3")
-        neg_mu = keep.tile([P, TILES], F32, name="neg_mu")
 
         def channel_constants():
             nc.vector.tensor_tensor(out=sq[:], in0=rs_sb[:], in1=rs_sb[:], op=MULT)
-            nc.vector.tensor_scalar(out=neg_mu[:], in0=mu_sb[:], scalar1=-1.0, scalar2=None, op0=MULT)
             nc.vector.scalar_tensor_tensor(out=c3[:], in0=sq[:], scalar=-1.0 / N, in1=rs_sb[:], op0=MULT, op1=MULT)
-            nc.vector.scalar_tensor_tensor(out=e3[:], in0=c3[:], scalar=float(N), in1=mu_sb[:], op0=MULT, op1=MULT)
 
         w_codes = keep.tile([P, CI], U32, name="w_codes", align_bytes=64)
         w_scales = keep.tile([P, CI], U8, name="w_scales", align_bytes=64)
@@ -139,7 +135,6 @@ def tile_adaattn3dstylizer_pa_v_kernel(tc, q, Wq, bq, mu, rstd, grad_out, out_0,
             nc.vector.quantize_mx(out=codes[:].bitcast(fmt), scales=scales[:], in_=grouped[(kind, b, h)][:].rearrange("p c t -> p (c t)"))
 
         neg_m1 = {}
-        d3 = {}
         r1 = {}
 
         acc_of = {}
@@ -165,16 +160,11 @@ def tile_adaattn3dstylizer_pa_v_kernel(tc, q, Wq, bq, mu, rstd, grad_out, out_0,
                 nc.tensor.matmul(out=neg_m1[b][:, j : j + 1], lhsT=part_of[b][:, j * P : (j + 1) * P], rhs=neg_inv_n[:], start=True, stop=True)
 
         def mean_terms(b):
-            cols = slice(b * J, (b + 1) * J)
-            d3[b] = work.tile([P, J], F32, name="d3", bufs=2)
             r1[b] = work.tile([P, J], F32, name="r1", bufs=2)
-            nc.vector.tensor_tensor(out=d3[b][:], in0=neg_m1[b][:], in1=e3[:, cols], op=MULT)
-            nc.vector.tensor_tensor(out=r1[b][:], in0=neg_m1[b][:], in1=rs_sb[:, cols], op=MULT)
+            nc.vector.tensor_tensor(out=r1[b][:], in0=neg_m1[b][:], in1=rs_sb[:, b * J : (b + 1) * J], op=MULT)
 
         dxn = {}
         s2 = {}
-        ab = {}
-        lin = {}
 
         def project(t):
             b, j = divmod(t, J)
@@ -185,43 +175,45 @@ def tile_adaattn3dstylizer_pa_v_kernel(tc, q, Wq, bq, mu, rstd, grad_out, out_0,
                                     start=True, stop=True)
                 dxn[(t, h)] = d
 
-        def second_moment(t):
-            b, j = divmod(t, J)
-            s2[t] = work.tile([P, 2], F32, name="s2")
-            for h in range(2):
-                junk = work.tile([P, HALF], F32, name="junk", bufs=2)
-                nc.vector.scalar_tensor_tensor(out=junk[:], in0=dxn[(t, h)][:], scalar=c3[:, t : t + 1], in1=q_sb[b][:, j, h * HALF : (h + 1) * HALF],
-                                               op0=MULT, op1=MULT, accum_out=s2[t][:, h : h + 1])
+        centred = {}
+        base = {}
+        slope = {}
 
-        def line(t):
+        def centre(t):
             b, j = divmod(t, J)
-            ab[t] = work.tile([P, 2], F32, name="ab")
-            nc.gpsimd.tensor_scalar(out=ab[t][:, 0:1], in0=s2[t][:, 0:1], scalar1=s2[t][:, 1:2], scalar2=d3[b][:, j : j + 1], op0=ADD, op1=ADD)
-            nc.gpsimd.tensor_scalar(out=ab[t][:, 1:2], in0=ab[t][:, 0:1], scalar1=neg_mu[:, t : t + 1], scalar2=r1[b][:, j : j + 1], op0=MULT, op1=ADD)
+            centred[t] = work.tile([P, N], F32, name="centred", bufs=3)
+            nc.gpsimd.tensor_scalar(out=centred[t][:], in0=q_sb[b][:, j, :], scalar1=mu_sb[:, t : t + 1], scalar2=0.0, op0=SUB, op1=ADD)
 
-        def linear_term(t, halves="SS"):
-            b, j = divmod(t, J)
-            lin[t] = work.tile([P, N], F32, name="lin")
-            if halves == "SS":
-                nc.scalar.activation(out=lin[t][:], in_=q_sb[b][:, j, :], func=IDENT, scale=ab[t][:, 0:1], bias=ab[t][:, 1:2])
-            else:
-                for h, e in enumerate(halves):
-                    cols = slice(h * HALF, (h + 1) * HALF)
-                    if e == "S":
-                        nc.scalar.activation(out=lin[t][:, cols], in_=q_sb[b][:, j, cols], func=IDENT, scale=ab[t][:, 0:1], bias=ab[t][:, 1:2])
-                    else:
-                        nc.vector.tensor_scalar(out=lin[t][:, cols], in0=q_sb[b][:, j, cols], scalar1=ab[t][:, 0:1], scalar2=ab[t][:, 1:2], op0=MULT, op1=ADD)
+        def moment_half(t, h):
+            if t not in s2:
+                s2[t] = work.tile([P, 2], F32, name="s2")
+            junk = work.tile([P, HALF], F32, name="junk", bufs=2)
+            nc.vector.scalar_tensor_tensor(out=junk[:], in0=dxn[(t, h)][:], scalar=c3[:, t : t + 1], in1=centred[t][:, h * HALF : (h + 1) * HALF],
+                                           op0=MULT, op1=MULT, accum_out=s2[t][:, h : h + 1])
 
-        def finish(t, split=False):
+        def base_half(t, h):
             b, j = divmod(t, J)
-            res = work.tile([P, N], F32, name="res")
+            if t not in base:
+                base[t] = work.tile([P, N], F32, name="base")
+            nc.scalar.activation(out=base[t][:, h * HALF : (h + 1) * HALF], in_=dxn[(t, h)][:], func=IDENT, scale=rs_sb[:, t : t + 1], bias=r1[b][:, j : j + 1])
+
+        def add_halves(t):
+            slope[t] = work.tile([P, 1], F32, name="slope")
+            nc.vector.tensor_tensor(out=slope[t][:], in0=s2[t][:, 0:1], in1=s2[t][:, 1:2], op=ADD)
+
+        res_of = {}
+
+        def finish_half(t, h, split=False):
+            b, j = divmod(t, J)
+            if t not in res_of:
+                res_of[t] = work.tile([P, N], F32, name="res")
+            res = res_of[t]
             out_rows = out_0[b].rearrange("(p j) n -> p j n", j=J)[:, j, :]
-            for h in range(2):
-                cols = slice(h * HALF, (h + 1) * HALF)
-                nc.vector.scalar_tensor_tensor(out=res[:, cols], in0=dxn[(t, h)][:], scalar=rs_sb[:, t : t + 1], in1=lin[t][:, cols], op0=MULT, op1=ADD)
-                if split:
-                    nc.sync.dma_start(out=out_rows[:, cols], in_=res[:, cols])
-            if not split:
+            cols = slice(h * HALF, (h + 1) * HALF)
+            nc.vector.scalar_tensor_tensor(out=res[:, cols], in0=centred[t][:, cols], scalar=slope[t][:], in1=base[t][:, cols], op0=MULT, op1=ADD)
+            if split:
+                nc.sync.dma_start(out=out_rows[:, cols], in_=res[:, cols])
+            elif h == 1:
                 nc.sync.dma_start(out=out_rows, in_=res[:])
 
         wacc = {}
@@ -245,10 +237,17 @@ def tile_adaattn3dstylizer_pa_v_kernel(tc, q, Wq, bq, mu, rstd, grad_out, out_0,
                 nc.tensor.matmul_mx(out=spare[:], lhsT=w_codes[:, 0:P].bitcast(E4), lhsT_scale=w_scales[:, 0:P],
                                     rhs=go_codes[0][:, 0:HALF].bitcast(E5), rhs_scale=go_scales[0][:, 0:HALF], start=True, stop=True)
 
+        def warm_up(n):
+            spare = psum_d.tile([P, P], F32, name="d")
+            for k in range(n):
+                nc.tensor.matmul(out=spare[:], lhsT=ident[:], rhs=ident[:], start=True, stop=True)
+
         interleave_g("V", 0, 0, 0, V_COLS)
         interleave_g("S", 0, 0, V_COLS, HALF)
+        warm_up(4)
         transpose_pair("g", 0, 0, 0)
         transpose_pair("g", 0, 0, 1)
+        warm_up(2)
         interleave_w("V", 0, 3)
         interleave_w("S", 3, 4)
         quantize_go(0, 0)
@@ -259,23 +258,25 @@ def tile_adaattn3dstylizer_pa_v_kernel(tc, q, Wq, bq, mu, rstd, grad_out, out_0,
         transpose_pair("g", 0, 1, 0)
         copy_pair("S", "g", 0, 0, 1)
         transpose_pair("g", 0, 1, 1)
+        warm_up(1)
+        for t in range(3):
+            centre(t)
         sum_products(0, (0, 1))
         quantize_go(0, 1)
+        project(0)
         sum_products(0, (2, 3))
         copy_pair("S", "g", 0, 1, 0)
         copy_pair("S", "g", 0, 1, 1)
-        project(0)
+        project(1)
         make_x(0, 0)
         make_x(0, 1)
         quantize_t("g", 0, 0)
+        channel_constants()
         make_x(0, 2)
         make_x(0, 3)
-        channel_constants()
         quantize_t("g", 0, 1)
         copy_sums(0)
-        interleave_g("V", 1, 0, 0, HALF)
         interleave_g("S", 1, 1, 0, HALF // 2)
-        project(1)
         transpose_pair("x", 0, 0, 0)
         mean(0)
         transpose_pair("x", 0, 0, 1)
@@ -286,55 +287,42 @@ def tile_adaattn3dstylizer_pa_v_kernel(tc, q, Wq, bq, mu, rstd, grad_out, out_0,
         quarters = {0: [(1, 3)], 1: [(2, 0)], 2: [(2, 1)], 3: [(2, 2)], 4: [(2, 3)]}
         quantize_at = {0: (1, 0), 1: (1, 1), 3: (2, 0), 5: (2, 1)}
         x_at = {0: (1, 0), 2: (1, 2), 4: (2, 0), 5: (2, 2)}
-        lin_e = ["SS"] * 11 + ["SV"]
         wg_at = {8: [0], 9: [1], 10: [2], 11: [3]}
         swg_at = {9: [0], 10: [1], 11: [2]}
         for t in range(TILES):
             b, j = divmod(t, J)
-            units = turn_at.get(t, [])
-            for n, (unit, pair) in enumerate([(unit, pair) for unit in units for pair in range(2)]):
-                if n < 1 or t == 0:
-                    transpose_pair(*unit, pair)
-                    if t > 0:
-                        copy_pair("S", *unit, pair)
-                if n == 0 and t > 0 and b + 1 < B:
-                    sum_products(b + 1, (j,))
-            if t in range(8):
+            pairs = [(unit, pair) for unit in turn_at.get(t, []) for pair in range(2)]
+            last = t == TILES - 1
+            for unit, pair in pairs[:1]:
+                transpose_pair(*unit, pair)
+            if t > 0 and b + 1 < B:
+                sum_products(b + 1, (j,))
+            if t in range(1, 8):
                 keep_clock(1)
-            second_moment(t)
+            moment_half(t, 0)
+            moment_half(t, 1)
+            for unit, pair in pairs[:1]:
+                copy_pair("S", *unit, pair)
             if t == 0:
+                interleave_g("V", 1, 0, 0, HALF)
+                quantize_t("x", 0, 0)
                 quantize_go(1, 0)
                 sum_products(1, (0,))
                 make_x(1, 0)
                 make_x(1, 1)
-            if t > 0 and j == 0:
-                finish(t - 1)
             if j == 0:
                 mean_terms(b)
-            line(t)
-            if j > 0:
-                finish(t - 1)
             if b + 1 < B and j == 3:
                 copy_sums(b + 1)
-            linear_term(t, lin_e[t])
-            if t == 0:
-                for unit in units:
-                    for pair in range(2):
-                        copy_pair("S", *unit, pair)
-            for gb, k in quarters.get(t, []):
-                interleave_g("S", gb, k // 2, (k % 2) * HALF // 2, (k % 2 + 1) * HALF // 2)
-            if 0 < t < TILES - 1:
-                project(t + 1)
-            if t in range(1, 8):
-                keep_clock(1)
-            for unit, pair in [(unit, pair) for unit in units for pair in range(2)][1:]:
-                if t > 0:
-                    transpose_pair(*unit, pair)
-                    copy_pair("S", *unit, pair)
+            base_half(t, 0)
+            base_half(t, 1)
+            for unit, pair in pairs[1:]:
+                transpose_pair(*unit, pair)
+                copy_pair("S", *unit, pair)
             if b + 1 < B and j == 3:
                 mean(b + 1)
-            if t == 1:
-                quantize_t("x", 0, 0)
+            for gb, k in quarters.get(t, []):
+                interleave_g("S", gb, k // 2, (k % 2) * HALF // 2, (k % 2 + 1) * HALF // 2)
             for unit in turn_at.get(t - 1, []):
                 quantize_t(*unit)
             if t in quantize_at and t > 0:
@@ -343,9 +331,19 @@ def tile_adaattn3dstylizer_pa_v_kernel(tc, q, Wq, bq, mu, rstd, grad_out, out_0,
                 xb, xj = x_at[t]
                 make_x(xb, xj)
                 make_x(xb, xj + 1)
+            if t > 0:
+                finish_half(t - 1, 0)
+            add_halves(t)
+            if t > 0:
+                finish_half(t - 1, 1)
+            if 0 < t and t + 2 < TILES:
+                centre(t + 2)
+            if t + 2 < TILES:
+                project(t + 2)
             for k in wg_at.get(t, []):
                 weight_grad(k)
             for k in swg_at.get(t, []):
                 store_weight_grad("S", k)
-        finish(TILES - 1, split=True)
+        finish_half(TILES - 1, 0, split=True)
+        finish_half(TILES - 1, 1, split=True)
         store_weight_grad("S", 3)

@@ -22,7 +22,7 @@ P = 128
 J = 4
 HALF = 512
 TILES = B * J
-V_COLS = 320
+V_COLS = 256
 
 
 def tile_adaattn3dstylizer_pa_v_kernel(tc, q, Wq, bq, mu, rstd, grad_out, out_0, out_1):
@@ -45,19 +45,26 @@ def tile_adaattn3dstylizer_pa_v_kernel(tc, q, Wq, bq, mu, rstd, grad_out, out_0,
             g_half[b] = g_all
         q_sb = [keep.tile([P, J, N], BF16, name="q%d" % b, align_bytes=64) for b in range(B)]
         w_sb = keep.tile([P, J, CI], BF16, name="w_sb", align_bytes=64)
-        mu_sb = keep.tile([P, TILES], F32, name="mu_sb")
-        rs_sb = keep.tile([P, TILES], F32, name="rs_sb")
+        stats_sb = keep.tile([P, 2 * TILES], F32, name="stats_sb")
+        mu_sb = stats_sb[:, 0:TILES]
+        rs_sb = stats_sb[:, TILES : 2 * TILES]
         g_view = [grad_out[b].rearrange("(p j) n -> p j n", j=J) for b in range(B)]
-        q_view = [q[b].rearrange("(p j) n -> p j n", j=J) for b in range(B)]
-        nc.sync.dma_start(out=g_half[(0, 0)][:], in_=g_view[0][:, :, 0:HALF])
+        q_view = [q[b].rearrange("(j p) n -> p j n", j=J) for b in range(B)]
+        stats = keep.tile([P, P], F32, name="stats")
+        nc.sync.dma_start(out=g_half[(0, 0)][:, :, 0 : HALF // 2], in_=g_view[0][:, :, 0 : HALF // 2])
+        nc.sync.dma_start(out=stats[0:TILES, :], in_=mu.rearrange("b (j p) -> (b j) p", p=P))
+        nc.sync.dma_start(out=stats[TILES : 2 * TILES, :], in_=rstd.rearrange("b (j p) -> (b j) p", p=P))
+        nc.sync.dma_start(out=stats[2 * TILES : 32, :], in_=mu[0:2, :].rearrange("b (j p) -> (b j) p", p=P))
+        nc.sync.dma_start(out=g_half[(0, 0)][:, :, HALF // 2 : HALF], in_=g_view[0][:, :, HALF // 2 : HALF])
         nc.sync.dma_start(out=w_sb[:], in_=Wq.rearrange("(p j) i -> p j i", j=J))
         nc.sync.dma_start(out=g_half[(0, 1)][:], in_=g_view[0][:, :, HALF:N])
-        nc.sync.dma_start(out=rs_sb[:].rearrange("p (b j) -> p b j", j=J), in_=rstd.rearrange("b (p j) -> p b j", j=J))
-        nc.sync.dma_start(out=mu_sb[:].rearrange("p (b j) -> p b j", j=J), in_=mu.rearrange("b (p j) -> p b j", j=J))
         nc.sync.dma_start(out=q_sb[0][:], in_=q_view[0])
         for b in range(1, B):
             nc.sync.dma_start(out=g_half[b][:], in_=g_view[b])
             nc.sync.dma_start(out=q_sb[b][:], in_=q_view[b])
+
+        nc.vector.memset(stats[32:64, :], 0.0)
+        nc.vector.memset(stats[64:P, :], 0.0)
 
         warm = keep.tile([P, 1], F32, name="warm")
         nc.vector.memset(warm[:], 0.0)
@@ -68,10 +75,21 @@ def tile_adaattn3dstylizer_pa_v_kernel(tc, q, Wq, bq, mu, rstd, grad_out, out_0,
         make_identity(nc, ident[:])
         sq = keep.tile([P, TILES], F32, name="sq")
         c3 = keep.tile([P, TILES], F32, name="c3")
+        e3 = keep.tile([P, TILES], F32, name="e3")
+        neg_mu = keep.tile([P, TILES], F32, name="neg_mu")
+
+        def turn_statistics():
+            stats_t = psum_t.tile([P, P], F32, name="bank")
+            nc.tensor.transpose(stats_t[:], stats[:], ident[:])
+            nc.scalar.copy(out=stats_sb[:], in_=stats_t[:, 0 : 2 * TILES])
 
         def channel_constants():
-            nc.vector.tensor_tensor(out=sq[:], in0=rs_sb[:], in1=rs_sb[:], op=MULT)
-            nc.vector.scalar_tensor_tensor(out=c3[:], in0=sq[:], scalar=-1.0 / N, in1=rs_sb[:], op0=MULT, op1=MULT)
+            nc.vector.tensor_tensor(out=sq[:], in0=rs_sb, in1=rs_sb, op=MULT)
+            nc.vector.tensor_scalar(out=neg_mu[:], in0=mu_sb, scalar1=-1.0, scalar2=None, op0=MULT)
+            nc.vector.scalar_tensor_tensor(out=c3[:], in0=sq[:], scalar=-1.0 / N, in1=rs_sb, op0=MULT, op1=MULT)
+
+        def channel_constants_2():
+            nc.vector.scalar_tensor_tensor(out=e3[:], in0=c3[:], scalar=float(N), in1=mu_sb, op0=MULT, op1=MULT)
 
         w_codes = keep.tile([P, CI], U32, name="w_codes", align_bytes=64)
         w_scales = keep.tile([P, CI], U8, name="w_scales", align_bytes=64)
@@ -90,6 +108,11 @@ def tile_adaattn3dstylizer_pa_v_kernel(tc, q, Wq, bq, mu, rstd, grad_out, out_0,
             else:
                 nc.scalar.copy(out=out, in_=in_)
 
+        def warm_up(n):
+            spare = psum_d.tile([P, HALF], F32, name="d")
+            for k in range(n):
+                nc.tensor.matmul(out=spare[:, 0:P], lhsT=ident[:], rhs=ident[:], start=True, stop=True)
+
         def interleave_g(engine, b, h, c0, c1):
             if (b, h) not in grouped:
                 grouped[(b, h)] = work.tile([P, HALF, J], BF16, name="go", bufs=2, align_bytes=64)
@@ -102,10 +125,10 @@ def tile_adaattn3dstylizer_pa_v_kernel(tc, q, Wq, bq, mu, rstd, grad_out, out_0,
             nc.vector.quantize_mx(out=go_codes[b][:, cols].bitcast(E5), scales=go_scales[b][:, cols],
                                   in_=grouped[(b, h)][:].rearrange("p c t -> p (c t)"))
 
-        w_grouped = keep.tile([P, J, P, J], BF16, name="w_grouped", align_bytes=64)
+        w_grouped = keep.tile([P, CI, J], BF16, name="w_grouped", align_bytes=64)
 
-        def interleave_w(engine, j0, j1):
-            copy(engine, w_grouped[:, j0:j1], w_sb[:].rearrange("p t (m j) -> p j m t", j=J)[:, j0:j1])
+        def interleave_w(engine, c0, c1):
+            copy(engine, w_grouped[:, c0:c1, :].rearrange("p (c i) t -> p c t i", i=4), w_sb[:, :, c0:c1].rearrange("p t (c i) -> p c t i", i=4))
 
         def make_x(b, j):
             if b not in x_sb:
@@ -135,9 +158,10 @@ def tile_adaattn3dstylizer_pa_v_kernel(tc, q, Wq, bq, mu, rstd, grad_out, out_0,
             nc.vector.quantize_mx(out=codes[:].bitcast(fmt), scales=scales[:], in_=grouped[(kind, b, h)][:].rearrange("p c t -> p (c t)"))
 
         neg_m1 = {}
+        d3 = {}
         r1 = {}
-
         acc_of = {}
+        part_of = {}
 
         def sum_products(b, pairs):
             for i in pairs:
@@ -147,8 +171,6 @@ def tile_adaattn3dstylizer_pa_v_kernel(tc, q, Wq, bq, mu, rstd, grad_out, out_0,
                     cols = slice(k * P, (k + 1) * P)
                     nc.tensor.matmul_mx(out=acc_of[b][:], lhsT=go_codes[b][:, cols].bitcast(E5), lhsT_scale=go_scales[b][:, cols],
                                         rhs=w_codes[:].bitcast(E4), rhs_scale=w_scales[:], start=(k == 0), stop=(k == 2 * J - 1))
-
-        part_of = {}
 
         def copy_sums(b):
             part_of[b] = work.tile([P, CI], F32, name="part", bufs=1)
@@ -160,8 +182,11 @@ def tile_adaattn3dstylizer_pa_v_kernel(tc, q, Wq, bq, mu, rstd, grad_out, out_0,
                 nc.tensor.matmul(out=neg_m1[b][:, j : j + 1], lhsT=part_of[b][:, j * P : (j + 1) * P], rhs=neg_inv_n[:], start=True, stop=True)
 
         def mean_terms(b):
+            cols = slice(b * J, (b + 1) * J)
+            d3[b] = work.tile([P, J], F32, name="d3", bufs=2)
             r1[b] = work.tile([P, J], F32, name="r1", bufs=2)
-            nc.vector.tensor_tensor(out=r1[b][:], in0=neg_m1[b][:], in1=rs_sb[:, b * J : (b + 1) * J], op=MULT)
+            nc.vector.tensor_tensor(out=d3[b][:], in0=neg_m1[b][:], in1=e3[:, cols], op=MULT)
+            nc.vector.tensor_tensor(out=r1[b][:], in0=neg_m1[b][:], in1=rs_sb[:, cols], op=MULT)
 
         dxn = {}
         s2 = {}
@@ -175,42 +200,46 @@ def tile_adaattn3dstylizer_pa_v_kernel(tc, q, Wq, bq, mu, rstd, grad_out, out_0,
                                     start=True, stop=True)
                 dxn[(t, h)] = d
 
-        centred = {}
-        base = {}
         slope = {}
+        offset = {}
+        lin = {}
 
-        def centre(t):
+        def moment(t):
             b, j = divmod(t, J)
-            centred[t] = work.tile([P, N], F32, name="centred", bufs=3)
-            nc.gpsimd.tensor_scalar(out=centred[t][:], in0=q_sb[b][:, j, :], scalar1=mu_sb[:, t : t + 1], scalar2=0.0, op0=SUB, op1=ADD)
+            s2[t] = work.tile([P, 2], F32, name="s2")
+            for h in range(2):
+                junk = work.tile([P, HALF], F32, name="junk", bufs=2)
+                nc.vector.scalar_tensor_tensor(out=junk[:], in0=dxn[(t, h)][:], scalar=c3[:, t : t + 1], in1=q_sb[b][:, j, h * HALF : (h + 1) * HALF],
+                                               op0=MULT, op1=MULT, accum_out=s2[t][:, h : h + 1])
 
-        def moment_half(t, h):
-            if t not in s2:
-                s2[t] = work.tile([P, 2], F32, name="s2")
-            junk = work.tile([P, HALF], F32, name="junk", bufs=2)
-            nc.vector.scalar_tensor_tensor(out=junk[:], in0=dxn[(t, h)][:], scalar=c3[:, t : t + 1], in1=centred[t][:, h * HALF : (h + 1) * HALF],
-                                           op0=MULT, op1=MULT, accum_out=s2[t][:, h : h + 1])
-
-        def base_half(t, h):
+        def slope_of(t):
             b, j = divmod(t, J)
-            if t not in base:
-                base[t] = work.tile([P, N], F32, name="base")
-            nc.scalar.activation(out=base[t][:, h * HALF : (h + 1) * HALF], in_=dxn[(t, h)][:], func=IDENT, scale=rs_sb[:, t : t + 1], bias=r1[b][:, j : j + 1])
-
-        def add_halves(t):
             slope[t] = work.tile([P, 1], F32, name="slope")
-            nc.vector.tensor_tensor(out=slope[t][:], in0=s2[t][:, 0:1], in1=s2[t][:, 1:2], op=ADD)
+            nc.vector.tensor_scalar(out=slope[t][:], in0=s2[t][:, 0:1], scalar1=s2[t][:, 1:2], scalar2=d3[b][:, j : j + 1], op0=ADD, op1=ADD)
+
+        def linear_term(t, engines="S"):
+            b, j = divmod(t, J)
+            offset[t] = work.tile([P, 1], F32, name="offset")
+            nc.scalar.activation(out=offset[t][:], in_=slope[t][:], func=IDENT, scale=neg_mu[:, t : t + 1], bias=r1[b][:, j : j + 1])
+            lin[t] = work.tile([P, N], F32, name="lin")
+            width = N // len(engines)
+            for k, e in enumerate(engines):
+                cols = slice(k * width, (k + 1) * width)
+                if e == "S":
+                    nc.scalar.activation(out=lin[t][:, cols], in_=q_sb[b][:, j, cols], func=IDENT, scale=slope[t][:], bias=offset[t][:])
+                else:
+                    nc.vector.tensor_scalar(out=lin[t][:, cols], in0=q_sb[b][:, j, cols], scalar1=slope[t][:], scalar2=offset[t][:], op0=MULT, op1=ADD)
 
         res_of = {}
 
         def finish_half(t, h, split=False):
             b, j = divmod(t, J)
-            if t not in res_of:
+            if h == 0:
                 res_of[t] = work.tile([P, N], F32, name="res")
             res = res_of[t]
-            out_rows = out_0[b].rearrange("(p j) n -> p j n", j=J)[:, j, :]
+            out_rows = out_0[b].rearrange("(j p) n -> p j n", j=J)[:, j, :]
             cols = slice(h * HALF, (h + 1) * HALF)
-            nc.vector.scalar_tensor_tensor(out=res[:, cols], in0=centred[t][:, cols], scalar=slope[t][:], in1=base[t][:, cols], op0=MULT, op1=ADD)
+            nc.vector.scalar_tensor_tensor(out=res[:, cols], in0=dxn[(t, h)][:], scalar=rs_sb[:, t : t + 1], in1=lin[t][:, cols], op0=MULT, op1=ADD)
             if split:
                 nc.sync.dma_start(out=out_rows[:, cols], in_=res[:, cols])
             elif h == 1:
@@ -228,118 +257,104 @@ def tile_adaattn3dstylizer_pa_v_kernel(tc, q, Wq, bq, mu, rstd, grad_out, out_0,
 
         def store_weight_grad(engine, j):
             res = work.tile([P, CI], F32, name="wres", bufs=4)
-            copy(engine, res[:].rearrange("p (m j) -> p m j", j=J), wacc[j][:].rearrange("p (j m) -> p m j", j=J))
+            copy(engine, res[:], wacc[j][:])
             nc.sync.dma_start(out=out_1.rearrange("(p j) i -> p j i", j=J)[:, j, :], in_=res[:])
 
-        def keep_clock(n):
-            spare = psum_t.tile([P, HALF], F32, name="bank")
-            for k in range(n):
-                nc.tensor.matmul_mx(out=spare[:], lhsT=w_codes[:, 0:P].bitcast(E4), lhsT_scale=w_scales[:, 0:P],
-                                    rhs=go_codes[0][:, 0:HALF].bitcast(E5), rhs_scale=go_scales[0][:, 0:HALF], start=True, stop=True)
-
-        def warm_up(n):
-            spare = psum_d.tile([P, P], F32, name="d")
-            for k in range(n):
-                nc.tensor.matmul(out=spare[:], lhsT=ident[:], rhs=ident[:], start=True, stop=True)
-
-        interleave_g("V", 0, 0, 0, V_COLS)
-        interleave_g("S", 0, 0, V_COLS, HALF)
-        warm_up(4)
+        interleave_g("V", 0, 0, 0, 256)
+        interleave_g("S", 0, 0, 256, HALF)
+        warm_up(2)
+        turn_statistics()
         transpose_pair("g", 0, 0, 0)
         transpose_pair("g", 0, 0, 1)
         warm_up(2)
-        interleave_w("V", 0, 3)
-        interleave_w("S", 3, 4)
+        interleave_w("V", 0, 448)
+        interleave_w("S", 448, CI)
         quantize_go(0, 0)
         copy_pair("S", "g", 0, 0, 0)
-        interleave_g("V", 0, 1, 0, V_COLS)
-        interleave_g("S", 0, 1, V_COLS, HALF)
-        nc.vector.quantize_mx(out=w_codes[:].bitcast(E4), scales=w_scales[:], in_=w_grouped[:].rearrange("p j m t -> p (j m t)"))
-        transpose_pair("g", 0, 1, 0)
+        interleave_g("V", 0, 1, 0, 320)
+        interleave_g("S", 0, 1, 320, HALF)
+        nc.vector.quantize_mx(out=w_codes[:].bitcast(E4), scales=w_scales[:], in_=w_grouped[:].rearrange("p c t -> p (c t)"))
         copy_pair("S", "g", 0, 0, 1)
-        transpose_pair("g", 0, 1, 1)
-        warm_up(1)
-        for t in range(3):
-            centre(t)
+        transpose_pair("g", 0, 1, 0)
         sum_products(0, (0, 1))
+        channel_constants()
         quantize_go(0, 1)
+        channel_constants_2()
         project(0)
         sum_products(0, (2, 3))
-        copy_pair("S", "g", 0, 1, 0)
-        copy_pair("S", "g", 0, 1, 1)
-        project(1)
         make_x(0, 0)
         make_x(0, 1)
+        transpose_pair("g", 0, 1, 1)
+        copy_sums(0)
+        copy_pair("S", "g", 0, 1, 0)
+        copy_pair("S", "g", 0, 1, 1)
         quantize_t("g", 0, 0)
-        channel_constants()
         make_x(0, 2)
         make_x(0, 3)
-        quantize_t("g", 0, 1)
-        copy_sums(0)
-        interleave_g("S", 1, 1, 0, HALF // 2)
-        transpose_pair("x", 0, 0, 0)
+        project(1)
         mean(0)
+        transpose_pair("x", 0, 0, 0)
         transpose_pair("x", 0, 0, 1)
+        interleave_g("S", 1, 1, 0, HALF // 2)
         copy_pair("S", "x", 0, 0, 0)
         copy_pair("S", "x", 0, 0, 1)
 
         turn_at = {0: [("x", 0, 1)], 1: [("g", 1, 0)], 2: [("g", 1, 1)], 3: [("x", 1, 0)], 4: [("x", 1, 1)], 5: [("g", 2, 0)], 6: [("g", 2, 1), ("x", 2, 0)], 7: [("x", 2, 1)]}
         quarters = {0: [(1, 3)], 1: [(2, 0)], 2: [(2, 1)], 3: [(2, 2)], 4: [(2, 3)]}
-        quantize_at = {0: (1, 0), 1: (1, 1), 3: (2, 0), 5: (2, 1)}
-        x_at = {0: (1, 0), 2: (1, 2), 4: (2, 0), 5: (2, 2)}
-        wg_at = {8: [0], 9: [1], 10: [2], 11: [3]}
+        quantize_at = {1: (1, 1), 3: (2, 0), 5: (2, 1)}
+        x_at = {1: [(1, 2)], 2: [(1, 3)], 3: [(2, 0)], 4: [(2, 1)], 5: [(2, 2), (2, 3)]}
+        sums_at = {0: (1, (0,)), 1: (1, (1,)), 2: (1, (2,)), 3: (1, (3,)), 4: (2, (0,)), 5: (2, (1,)), 6: (2, (2,)), 7: (2, (3,))}
+        wg_at = {8: [0], 9: [1], 10: [2, 3]}
         swg_at = {9: [0], 10: [1], 11: [2]}
         for t in range(TILES):
             b, j = divmod(t, J)
             pairs = [(unit, pair) for unit in turn_at.get(t, []) for pair in range(2)]
-            last = t == TILES - 1
-            for unit, pair in pairs[:1]:
+            early = 1
+            for unit, pair in pairs[:early]:
                 transpose_pair(*unit, pair)
-            if t > 0 and b + 1 < B:
-                sum_products(b + 1, (j,))
-            if t in range(1, 8):
-                keep_clock(1)
-            moment_half(t, 0)
-            moment_half(t, 1)
-            for unit, pair in pairs[:1]:
-                copy_pair("S", *unit, pair)
+                if t > 0:
+                    copy_pair("S", *unit, pair)
+            if t in sums_at and t > 0:
+                sum_products(*sums_at[t])
+            moment(t)
             if t == 0:
                 interleave_g("V", 1, 0, 0, HALF)
-                quantize_t("x", 0, 0)
-                quantize_go(1, 0)
-                sum_products(1, (0,))
-                make_x(1, 0)
-                make_x(1, 1)
-            if j == 0:
+                quantize_t("g", 0, 1)
+                mean_terms(0)
+            if t > 0:
+                finish_half(t - 1, 0)
+            if t > 0 and j == 0:
                 mean_terms(b)
+            slope_of(t)
+            if t > 0:
+                finish_half(t - 1, 1)
             if b + 1 < B and j == 3:
                 copy_sums(b + 1)
-            base_half(t, 0)
-            base_half(t, 1)
-            for unit, pair in pairs[1:]:
+            linear_term(t, "VS" if t == TILES - 1 else "S")
+            if t == 0:
+                for unit, pair in pairs[:early]:
+                    copy_pair("S", *unit, pair)
+            for gb, k in quarters.get(t, []):
+                interleave_g("S", gb, k // 2, (k % 2) * HALF // 2, (k % 2 + 1) * HALF // 2)
+            if 0 < t < TILES - 1:
+                project(t + 1)
+            for unit, pair in pairs[early:]:
                 transpose_pair(*unit, pair)
                 copy_pair("S", *unit, pair)
             if b + 1 < B and j == 3:
                 mean(b + 1)
-            for gb, k in quarters.get(t, []):
-                interleave_g("S", gb, k // 2, (k % 2) * HALF // 2, (k % 2 + 1) * HALF // 2)
+            if t == 0:
+                quantize_go(1, 0)
+                sum_products(*sums_at[t])
+                make_x(1, 0)
+                make_x(1, 1)
+                quantize_t("x", 0, 0)
+            for xb, xj in x_at.get(t, []):
+                make_x(xb, xj)
             for unit in turn_at.get(t - 1, []):
                 quantize_t(*unit)
-            if t in quantize_at and t > 0:
+            if t in quantize_at:
                 quantize_go(*quantize_at[t])
-            if t in x_at and t > 0:
-                xb, xj = x_at[t]
-                make_x(xb, xj)
-                make_x(xb, xj + 1)
-            if t > 0:
-                finish_half(t - 1, 0)
-            add_halves(t)
-            if t > 0:
-                finish_half(t - 1, 1)
-            if 0 < t and t + 2 < TILES:
-                centre(t + 2)
-            if t + 2 < TILES:
-                project(t + 2)
             for k in wg_at.get(t, []):
                 weight_grad(k)
             for k in swg_at.get(t, []):

from contextlib import ExitStack

import concourse.mybir as mybir
from concourse.masks import make_identity

B, CI, CO, N = 3, 512, 512, 1024
FLOPS = 2 * 2 * CO * CI * B * N
BYTES = 2 * (2 * B * CI * N + CO * CI) + 4 * (2 * B * CI + B * CI * N + CO * CI)

F32 = mybir.dt.float32
BF16 = mybir.dt.bfloat16
U32 = mybir.dt.uint32
U8 = mybir.dt.uint8
E4 = mybir.dt.float8_e4m3fn_x4
E5 = mybir.dt.float8_e5m2_x4
ADD = mybir.AluOpType.add
SUB = mybir.AluOpType.subtract
MULT = mybir.AluOpType.mult
IDENT = mybir.ActivationFunctionType.Identity

P = 128
J = 4
HALF = 512
TILES = B * J
V_COLS = 256


def tile_adaattn3dstylizer_pa_v_kernel(tc, q, Wq, bq, mu, rstd, grad_out, out_0, out_1):
    nc = tc.nc
    with ExitStack() as ctx:
        keep = ctx.enter_context(tc.tile_pool(name="keep", bufs=1))
        work = ctx.enter_context(tc.tile_pool(name="work", bufs=3))
        psum_d = ctx.enter_context(tc.psum_pool(name="psum_d", bufs=4))
        psum_t = ctx.enter_context(tc.psum_pool(name="psum_t", bufs=3))
        psum_s = ctx.enter_context(tc.psum_pool(name="psum_s", bufs=1))
        ctx.enter_context(tc.manual_schedule())

        g_half = {}
        for h in range(2):
            g_half[(0, h)] = keep.tile([P, J, HALF], BF16, name="g0%d" % h, align_bytes=64)
        for b in range(1, B):
            g_all = keep.tile([P, J, N], BF16, name="g%d" % b, align_bytes=64)
            for h in range(2):
                g_half[(b, h)] = g_all[:, :, h * HALF : (h + 1) * HALF]
            g_half[b] = g_all
        q_sb = [keep.tile([P, J, N], BF16, name="q%d" % b, align_bytes=64) for b in range(B)]
        w_sb = keep.tile([P, J, CI], BF16, name="w_sb", align_bytes=64)
        stats_sb = keep.tile([P, 2 * TILES], F32, name="stats_sb")
        mu_sb = stats_sb[:, 0:TILES]
        rs_sb = stats_sb[:, TILES : 2 * TILES]
        g_view = [grad_out[b].rearrange("(p j) n -> p j n", j=J) for b in range(B)]
        q_view = [q[b].rearrange("(j p) n -> p j n", j=J) for b in range(B)]
        stats = keep.tile([P, P], F32, name="stats")
        nc.sync.dma_start(out=g_half[(0, 0)][:, :, 0 : HALF // 2], in_=g_view[0][:, :, 0 : HALF // 2])
        nc.sync.dma_start(out=stats[0:TILES, :], in_=mu.rearrange("b (j p) -> (b j) p", p=P))
        nc.sync.dma_start(out=stats[TILES : 2 * TILES, :], in_=rstd.rearrange("b (j p) -> (b j) p", p=P))
        nc.sync.dma_start(out=stats[2 * TILES : 32, :], in_=mu[0:2, :].rearrange("b (j p) -> (b j) p", p=P))
        nc.sync.dma_start(out=g_half[(0, 0)][:, :, HALF // 2 : HALF], in_=g_view[0][:, :, HALF // 2 : HALF])
        nc.sync.dma_start(out=w_sb[:], in_=Wq.rearrange("(p j) i -> p j i", j=J))
        nc.sync.dma_start(out=g_half[(0, 1)][:], in_=g_view[0][:, :, HALF:N])
        nc.sync.dma_start(out=q_sb[0][:], in_=q_view[0])
        for b in range(1, B):
            nc.sync.dma_start(out=g_half[b][:], in_=g_view[b])
            nc.sync.dma_start(out=q_sb[b][:], in_=q_view[b])

        nc.vector.memset(stats[32:64, :], 0.0)
        nc.vector.memset(stats[64:P, :], 0.0)

        warm = keep.tile([P, 1], F32, name="warm")
        nc.vector.memset(warm[:], 0.0)
        nc.scalar.activation(out=warm[:], in_=warm[:], func=IDENT)
        neg_inv_n = keep.tile([P, 1], F32, name="neg_inv_n")
        nc.vector.memset(neg_inv_n[:], -1.0 / N)
        ident = keep.tile([P, P], F32, name="ident")
        make_identity(nc, ident[:])
        sq = keep.tile([P, TILES], F32, name="sq")
        c3 = keep.tile([P, TILES], F32, name="c3")
        e3 = keep.tile([P, TILES], F32, name="e3")
        neg_mu = keep.tile([P, TILES], F32, name="neg_mu")

        def turn_statistics():
            stats_t = psum_t.tile([P, P], F32, name="bank")
            nc.tensor.transpose(stats_t[:], stats[:], ident[:])
            nc.scalar.copy(out=stats_sb[:], in_=stats_t[:, 0 : 2 * TILES])

        def channel_constants():
            nc.vector.tensor_tensor(out=sq[:], in0=rs_sb, in1=rs_sb, op=MULT)
            nc.vector.tensor_scalar(out=neg_mu[:], in0=mu_sb, scalar1=-1.0, scalar2=None, op0=MULT)
            nc.vector.scalar_tensor_tensor(out=c3[:], in0=sq[:], scalar=-1.0 / N, in1=rs_sb, op0=MULT, op1=MULT)

        def channel_constants_2():
            nc.vector.scalar_tensor_tensor(out=e3[:], in0=c3[:], scalar=float(N), in1=mu_sb, op0=MULT, op1=MULT)

        w_codes = keep.tile([P, CI], U32, name="w_codes", align_bytes=64)
        w_scales = keep.tile([P, CI], U8, name="w_scales", align_bytes=64)
        go_codes = [keep.tile([P, N], U32, name="go_codes%d" % b, align_bytes=64) for b in range(B)]
        go_scales = [keep.tile([P, N], U8, name="go_scales%d" % b, align_bytes=64) for b in range(B)]
        gt_codes = [keep.tile([P, CO], U32, name="gt_codes%d" % k, align_bytes=64) for k in range(2 * B)]
        gt_scales = [keep.tile([P, CO], U8, name="gt_scales%d" % k, align_bytes=64) for k in range(2 * B)]
        xt_codes = [keep.tile([P, CI], U32, name="xt_codes%d" % k, align_bytes=64) for k in range(2 * B)]
        xt_scales = [keep.tile([P, CI], U8, name="xt_scales%d" % k, align_bytes=64) for k in range(2 * B)]
        x_sb = {}
        grouped = {}

        def copy(engine, out, in_):
            if engine == "V":
                nc.vector.tensor_copy(out=out, in_=in_)
            else:
                nc.scalar.copy(out=out, in_=in_)

        def warm_up(n):
            spare = psum_d.tile([P, HALF], F32, name="d")
            for k in range(n):
                nc.tensor.matmul(out=spare[:, 0:P], lhsT=ident[:], rhs=ident[:], start=True, stop=True)

        def interleave_g(engine, b, h, c0, c1):
            if (b, h) not in grouped:
                grouped[(b, h)] = work.tile([P, HALF, J], BF16, name="go", bufs=2, align_bytes=64)
            dst = grouped[(b, h)][:, c0:c1, :].rearrange("p (c i) t -> p c t i", i=4)
            src = g_half[(b, h)][:, :, c0:c1].rearrange("p t (c i) -> p c t i", i=4)
            copy(engine, dst, src)

        def quantize_go(b, h):
            cols = slice(h * HALF, (h + 1) * HALF)
            nc.vector.quantize_mx(out=go_codes[b][:, cols].bitcast(E5), scales=go_scales[b][:, cols],
                                  in_=grouped[(b, h)][:].rearrange("p c t -> p (c t)"))

        w_grouped = keep.tile([P, CI, J], BF16, name="w_grouped", align_bytes=64)

        def interleave_w(engine, c0, c1):
            copy(engine, w_grouped[:, c0:c1, :].rearrange("p (c i) t -> p c t i", i=4), w_sb[:, :, c0:c1].rearrange("p t (c i) -> p c t i", i=4))

        def make_x(b, j):
            if b not in x_sb:
                x_sb[b] = work.tile([P, J, N], BF16, name="x", bufs=2, align_bytes=64)
            col = slice(b * J + j, b * J + j + 1)
            nc.vector.tensor_scalar(out=x_sb[b][:, j, :], in0=q_sb[b][:, j, :], scalar1=mu_sb[:, col], scalar2=rs_sb[:, col], op0=SUB, op1=MULT)

        turned = {}

        def transpose_pair(kind, b, h, pair):
            bank = psum_t.tile([P, 2, 2, P], F32, name="bank")
            for jj in range(2):
                rows = g_half[(b, h)][:, 2 * pair + jj, :] if kind == "g" else x_sb[b][:, 2 * pair + jj, h * HALF : (h + 1) * HALF]
                for u in range(2):
                    nc.tensor.transpose(bank[:, jj, u, :], rows.bitcast(F32)[:, u::2], ident[:])
            turned[(kind, b, h, pair)] = bank

        def copy_pair(engine, kind, b, h, pair):
            if (kind, b, h) not in grouped:
                grouped[(kind, b, h)] = work.tile([P, CO, J], BF16, name="tt", bufs=4, align_bytes=64)
            dst = grouped[(kind, b, h)][:].rearrange("p c t -> p (c t)").bitcast(F32)[:, pair * 512 : (pair + 1) * 512]
            copy(engine, dst.rearrange("p (j r u) -> p j r u", j=2, u=2), turned[(kind, b, h, pair)][:].rearrange("p j u r -> p j r u"))

        def quantize_t(kind, b, h):
            k = 2 * b + h
            codes, scales, fmt = (gt_codes[k], gt_scales[k], E5) if kind == "g" else (xt_codes[k], xt_scales[k], E4)
            nc.vector.quantize_mx(out=codes[:].bitcast(fmt), scales=scales[:], in_=grouped[(kind, b, h)][:].rearrange("p c t -> p (c t)"))

        neg_m1 = {}
        d3 = {}
        r1 = {}
        acc_of = {}
        part_of = {}

        def sum_products(b, pairs):
            for i in pairs:
                if i == 0:
                    acc_of[b] = psum_s.tile([P, CI], F32, name="acc")
                for k in (2 * i, 2 * i + 1):
                    cols = slice(k * P, (k + 1) * P)
                    nc.tensor.matmul_mx(out=acc_of[b][:], lhsT=go_codes[b][:, cols].bitcast(E5), lhsT_scale=go_scales[b][:, cols],
                                        rhs=w_codes[:].bitcast(E4), rhs_scale=w_scales[:], start=(k == 0), stop=(k == 2 * J - 1))

        def copy_sums(b):
            part_of[b] = work.tile([P, CI], F32, name="part", bufs=1)
            nc.scalar.copy(out=part_of[b][:], in_=acc_of[b][:])

        def mean(b):
            neg_m1[b] = psum_s.tile([P, J], F32, name="acc")
            for j in range(J):
                nc.tensor.matmul(out=neg_m1[b][:, j : j + 1], lhsT=part_of[b][:, j * P : (j + 1) * P], rhs=neg_inv_n[:], start=True, stop=True)

        def mean_terms(b):
            cols = slice(b * J, (b + 1) * J)
            d3[b] = work.tile([P, J], F32, name="d3", bufs=2)
            r1[b] = work.tile([P, J], F32, name="r1", bufs=2)
            nc.vector.tensor_tensor(out=d3[b][:], in0=neg_m1[b][:], in1=e3[:, cols], op=MULT)
            nc.vector.tensor_tensor(out=r1[b][:], in0=neg_m1[b][:], in1=rs_sb[:, cols], op=MULT)

        dxn = {}
        s2 = {}

        def project(t):
            b, j = divmod(t, J)
            for h in range(2):
                d = psum_d.tile([P, HALF], F32, name="d")
                nc.tensor.matmul_mx(out=d[:], lhsT=w_codes[:, j * P : (j + 1) * P].bitcast(E4), lhsT_scale=w_scales[:, j * P : (j + 1) * P],
                                    rhs=go_codes[b][:, h * HALF : (h + 1) * HALF].bitcast(E5), rhs_scale=go_scales[b][:, h * HALF : (h + 1) * HALF],
                                    start=True, stop=True)
                dxn[(t, h)] = d

        slope = {}
        offset = {}
        lin = {}

        def moment(t):
            b, j = divmod(t, J)
            s2[t] = work.tile([P, 2], F32, name="s2")
            for h in range(2):
                junk = work.tile([P, HALF], F32, name="junk", bufs=2)
                nc.vector.scalar_tensor_tensor(out=junk[:], in0=dxn[(t, h)][:], scalar=c3[:, t : t + 1], in1=q_sb[b][:, j, h * HALF : (h + 1) * HALF],
                                               op0=MULT, op1=MULT, accum_out=s2[t][:, h : h + 1])

        def slope_of(t):
            b, j = divmod(t, J)
            slope[t] = work.tile([P, 1], F32, name="slope")
            nc.vector.tensor_scalar(out=slope[t][:], in0=s2[t][:, 0:1], scalar1=s2[t][:, 1:2], scalar2=d3[b][:, j : j + 1], op0=ADD, op1=ADD)

        def linear_term(t, engines="S"):
            b, j = divmod(t, J)
            offset[t] = work.tile([P, 1], F32, name="offset")
            nc.scalar.activation(out=offset[t][:], in_=slope[t][:], func=IDENT, scale=neg_mu[:, t : t + 1], bias=r1[b][:, j : j + 1])
            lin[t] = work.tile([P, N], F32, name="lin")
            width = N // len(engines)
            for k, e in enumerate(engines):
                cols = slice(k * width, (k + 1) * width)
                if e == "S":
                    nc.scalar.activation(out=lin[t][:, cols], in_=q_sb[b][:, j, cols], func=IDENT, scale=slope[t][:], bias=offset[t][:])
                else:
                    nc.vector.tensor_scalar(out=lin[t][:, cols], in0=q_sb[b][:, j, cols], scalar1=slope[t][:], scalar2=offset[t][:], op0=MULT, op1=ADD)

        res_of = {}

        def finish_half(t, h, split=False):
            b, j = divmod(t, J)
            if h == 0:
                res_of[t] = work.tile([P, N], F32, name="res")
            res = res_of[t]
            out_rows = out_0[b].rearrange("(j p) n -> p j n", j=J)[:, j, :]
            cols = slice(h * HALF, (h + 1) * HALF)
            nc.vector.scalar_tensor_tensor(out=res[:, cols], in0=dxn[(t, h)][:], scalar=rs_sb[:, t : t + 1], in1=lin[t][:, cols], op0=MULT, op1=ADD)
            if split:
                nc.sync.dma_start(out=out_rows[:, cols], in_=res[:, cols])
            elif h == 1:
                nc.sync.dma_start(out=out_rows, in_=res[:])

        wacc = {}

        def weight_grad(j):
            acc = psum_t.tile([P, CI], F32, name="bank")
            for k in range(2 * B):
                cols = slice(j * P, (j + 1) * P)
                nc.tensor.matmul_mx(out=acc[:], lhsT=gt_codes[k][:, cols].bitcast(E5), lhsT_scale=gt_scales[k][:, cols],
                                    rhs=xt_codes[k][:].bitcast(E4), rhs_scale=xt_scales[k][:], start=(k == 0), stop=(k == 2 * B - 1))
            wacc[j] = acc

        def store_weight_grad(engine, j):
            res = work.tile([P, CI], F32, name="wres", bufs=4)
            copy(engine, res[:], wacc[j][:])
            nc.sync.dma_start(out=out_1.rearrange("(p j) i -> p j i", j=J)[:, j, :], in_=res[:])

        interleave_g("V", 0, 0, 0, 256)
        interleave_g("S", 0, 0, 256, HALF)
        warm_up(2)
        turn_statistics()
        transpose_pair("g", 0, 0, 0)
        transpose_pair("g", 0, 0, 1)
        warm_up(2)
        interleave_w("V", 0, 448)
        interleave_w("S", 448, CI)
        quantize_go(0, 0)
        copy_pair("S", "g", 0, 0, 0)
        interleave_g("V", 0, 1, 0, 320)
        interleave_g("S", 0, 1, 320, HALF)
        nc.vector.quantize_mx(out=w_codes[:].bitcast(E4), scales=w_scales[:], in_=w_grouped[:].rearrange("p c t -> p (c t)"))
        copy_pair("S", "g", 0, 0, 1)
        transpose_pair("g", 0, 1, 0)
        sum_products(0, (0, 1))
        channel_constants()
        quantize_go(0, 1)
        channel_constants_2()
        project(0)
        sum_products(0, (2, 3))
        make_x(0, 0)
        make_x(0, 1)
        transpose_pair("g", 0, 1, 1)
        copy_sums(0)
        copy_pair("S", "g", 0, 1, 0)
        copy_pair("S", "g", 0, 1, 1)
        quantize_t("g", 0, 0)
        make_x(0, 2)
        make_x(0, 3)
        project(1)
        mean(0)
        transpose_pair("x", 0, 0, 0)
        transpose_pair("x", 0, 0, 1)
        interleave_g("S", 1, 1, 0, HALF // 2)
        copy_pair("S", "x", 0, 0, 0)
        copy_pair("S", "x", 0, 0, 1)

        turn_at = {0: [("x", 0, 1)], 1: [("g", 1, 0)], 2: [("g", 1, 1)], 3: [("x", 1, 0)], 4: [("x", 1, 1)], 5: [("g", 2, 0)], 6: [("g", 2, 1), ("x", 2, 0)], 7: [("x", 2, 1)]}
        quarters = {0: [(1, 3)], 1: [(2, 0)], 2: [(2, 1)], 3: [(2, 2)], 4: [(2, 3)]}
        quantize_at = {1: (1, 1), 3: (2, 0), 5: (2, 1)}
        x_at = {1: [(1, 2)], 2: [(1, 3)], 3: [(2, 0)], 4: [(2, 1)], 5: [(2, 2), (2, 3)]}
        sums_at = {0: (1, (0,)), 1: (1, (1,)), 2: (1, (2,)), 3: (1, (3,)), 4: (2, (0,)), 5: (2, (1,)), 6: (2, (2,)), 7: (2, (3,))}
        wg_at = {8: [0], 9: [1], 10: [2, 3]}
        swg_at = {9: [0], 10: [1], 11: [2]}
        for t in range(TILES):
            b, j = divmod(t, J)
            pairs = [(unit, pair) for unit in turn_at.get(t, []) for pair in range(2)]
            early = 1
            for unit, pair in pairs[:early]:
                transpose_pair(*unit, pair)
                if t > 0:
                    copy_pair("S", *unit, pair)
            if t in sums_at and t > 0:
                sum_products(*sums_at[t])
            moment(t)
            if t == 0:
                interleave_g("V", 1, 0, 0, HALF)
                quantize_t("g", 0, 1)
                mean_terms(0)
            if t > 0:
                finish_half(t - 1, 0)
            if t > 0 and j == 0:
                mean_terms(b)
            slope_of(t)
            if t > 0:
                finish_half(t - 1, 1)
            if b + 1 < B and j == 3:
                copy_sums(b + 1)
            linear_term(t, "VS" if t == TILES - 1 else "S")
            if t == 0:
                for unit, pair in pairs[:early]:
                    copy_pair("S", *unit, pair)
            for gb, k in quarters.get(t, []):
                interleave_g("S", gb, k // 2, (k % 2) * HALF // 2, (k % 2 + 1) * HALF // 2)
            if 0 < t < TILES - 1:
                project(t + 1)
            for unit, pair in pairs[early:]:
                transpose_pair(*unit, pair)
                copy_pair("S", *unit, pair)
            if b + 1 < B and j == 3:
                mean(b + 1)
            if t == 0:
                quantize_go(1, 0)
                sum_products(*sums_at[t])
                make_x(1, 0)
                make_x(1, 1)
                quantize_t("x", 0, 0)
            for xb, xj in x_at.get(t, []):
                make_x(xb, xj)
            for unit in turn_at.get(t - 1, []):
                quantize_t(*unit)
            if t in quantize_at:
                quantize_go(*quantize_at[t])
            for k in wg_at.get(t, []):
                weight_grad(k)
            for k in swg_at.get(t, []):
                store_weight_grad("S", k)
        finish_half(TILES - 1, 0, split=True)
        finish_half(TILES - 1, 1, split=True)
        store_weight_grad("S", 3)
